import numpy as np
import ml_dtypes


def mxq(x, axis, fmt="e4m3"):
    dtype, down = {"e4m3": (ml_dtypes.float8_e4m3fn, 7), "e5m2": (ml_dtypes.float8_e5m2, 14)}[fmt]
    v = np.moveaxis(np.asarray(x, np.float32).astype(ml_dtypes.bfloat16).astype(np.float64), axis, -1)
    blocks = v.reshape(v.shape[:-1] + (-1, 32))
    amax = np.abs(blocks).max(-1, keepdims=True)
    byte = np.maximum(np.where(amax > 0, np.frexp(amax)[1] - 1 + 127, 0) - down, 1)
    scale = np.exp2(byte - 127.0)
    codes = (blocks / scale).astype(np.float32).astype(dtype).astype(np.float64)
    return np.moveaxis((codes * scale).reshape(v.shape), -1, axis)


WIDE = False


def mx_kscale(k):
    if not WIDE:
        return np.ones(k)
    levels = np.array([10, -10, 5, -5, 0])
    a = np.random.permutation(np.resize(levels, k // 512 * 4)).reshape(k // 512, 4)
    idx = np.arange(k)
    return np.exp2(a[idx // 512, idx % 128 // 32])


BF16 = ml_dtypes.bfloat16


def bf(x):
    return np.asarray(x, np.float32).astype(BF16)


def f64(x):
    return np.asarray(x).astype(np.float64)


G, B, D, F, O = 4, 256, 512, 2048, 512


def silu(v):
    return v / (1.0 + np.exp(-v))


def setup_inputs():
    s, t = mx_kscale(D), mx_kscale(F)
    return {"x": bf(np.random.standard_normal((B * G, D)) * s),
            "gate_weight": bf(np.random.standard_normal((G, D, F)) / np.sqrt(D) / s[:, None]),
            "up_weight": bf(np.random.standard_normal((G, D, F)) / np.sqrt(D) / s[:, None] * t),
            "down_weight": bf(np.random.standard_normal((G, F, O)) * 1.5 / np.sqrt(F) / t[:, None])}


def reference(x, gate_weight, up_weight, down_weight):
    num_groups = gate_weight.shape[0]
    input_dim = gate_weight.shape[1]
    batch = x.shape[0] // num_groups
    xb = f64(x).reshape(batch, num_groups, input_dim)
    xq = mxq(xb, 2, "e4m3").transpose(1, 0, 2)
    gate = xq @ mxq(f64(gate_weight), 1, "e4m3")
    up = xq @ mxq(f64(up_weight), 1, "e4m3")
    hidden = silu(gate) * up
    out = mxq(hidden, 2, "e4m3") @ mxq(f64(down_weight), 1, "e4m3")
    return out.transpose(1, 0, 2).reshape(-1, down_weight.shape[-1])

@@ -1,0 +1,263 @@
+from contextlib import ExitStack
+
+import concourse.mybir as mybir
+from concourse.masks import make_identity
+
+BF16 = mybir.dt.bfloat16
+F32 = mybir.dt.float32
+U32 = mybir.dt.uint32
+U8 = mybir.dt.uint8
+FP8X4 = mybir.dt.float8_e4m3fn_x4
+SILU = mybir.ActivationFunctionType.Silu
+MULT = mybir.AluOpType.mult
+
+P = 128
+G = 4
+H = 2
+D = 512
+F = 2048
+O = 512
+C = 4
+W = 512
+NSTEP = G * C
+
+FLOPS = 2 * 1024 * D * F * 2 + 2 * 1024 * F * O
+
+VD = 216
+FIRST = 336
+RAW_BUFS = 6
+
+
+def split_of(n):
+    if n == 0:
+        return (FIRST, FIRST, VD)
+    return (W, 0, VD)
+
+
+def tile_groupedmlp_plana_kernel(tc, x, gate_weight, up_weight, down_weight, out):
+    nc = tc.nc
+    xv = x.rearrange("(h b g) d -> g b h d", h=H, g=G)
+    gv = gate_weight.rearrange("g (p j) f -> g p j f", j=4)
+    uv = up_weight.rearrange("g (p j) f -> g p j f", j=4)
+    dv = down_weight.rearrange("g (c t p) o -> g c p t o", c=C, t=4)
+    ov = out.rearrange("(h b g) o -> g h b o", h=H, g=G)
+
+    with ExitStack() as ctx:
+        const = ctx.enter_context(tc.tile_pool(name="const", bufs=1))
+        raw = ctx.enter_context(tc.tile_pool(name="raw", bufs=RAW_BUFS))
+        grp = ctx.enter_context(tc.tile_pool(name="grp", bufs=2))
+        cod = ctx.enter_context(tc.tile_pool(name="cod", bufs=3))
+        xs = ctx.enter_context(tc.tile_pool(name="xs", bufs=2))
+        hid = ctx.enter_context(tc.tile_pool(name="hid", bufs=2))
+        res = ctx.enter_context(tc.tile_pool(name="res", bufs=4))
+        psum = ctx.enter_context(tc.psum_pool(name="psum", bufs=3))
+        ctx.enter_context(tc.manual_schedule())
+
+        rawt = {}
+        xraw = {}
+        xbank = {}
+        xgrp = {}
+        xcodes = {}
+        grouped = {}
+        codes = {}
+        banks = {}
+        silus = {}
+        hgrp = {}
+        hcodes = {}
+        obanks = {}
+
+        def load_x(g):
+            xr = xs.tile([P, H, D], BF16, name="xr", tag="xr", bufs=G)
+            nc.sync.dma_start(out=xr[:], in_=xv[g])
+            xraw[g] = xr
+
+        def load_unit(n, k):
+            g, c = divmod(n, C)
+            rt = raw.tile([P, 4, W], BF16, name="raw%d" % k, tag="raw%d" % k)
+            if k == 2:
+                nc.sync.dma_start(out=rt[:], in_=dv[g, c])
+            else:
+                nc.sync.dma_start(out=rt[:], in_=(gv, uv)[k][g, :, :, c * W : (c + 1) * W])
+            rawt[(n, k)] = rt
+
+        def load_round(m):
+            if m < NSTEP:
+                load_unit(m, 0)
+                load_unit(m, 1)
+            if 1 <= m <= NSTEP:
+                load_unit(m - 1, 2)
+            if m % C == 1 and m // C + 1 < G:
+                load_x(m // C + 1)
+
+        def x_transposes(g):
+            words = xraw[g][:].bitcast(F32).rearrange("p h (w u) -> p h u w", u=2)
+            xt = psum.tile([P, H, 2, P], F32, name="xt", tag="ps0")
+            for h in range(H):
+                for u in range(2):
+                    nc.tensor.transpose(out=xt[:, h, u, :], in_=words[:, h, u, :], identity=ident[:])
+            xbank[g] = xt
+
+        def x_evac(g):
+            xg = xs.tile([P, H, P, 4], BF16, name="xg", tag="xg", align_bytes=64)
+            nc.scalar.copy(out=xg[:].bitcast(F32), in_=xbank[g][:].rearrange("p h u b -> p h b u"))
+            xgrp[g] = xg
+
+        def x_quant(g):
+            xc = xs.tile([P, H * P], U32, name="xc", tag="xc", align_bytes=64)
+            xsc = xs.tile([P, H * P], U8, name="xsc", tag="xsc", align_bytes=64)
+            nc.vector.quantize_mx(
+                out=xc[:].bitcast(FP8X4),
+                scales=xsc[:],
+                in_=xgrp[g][:].rearrange("p h b t -> p (h b t)"),
+            )
+            xcodes[g] = (xc, xsc)
+
+        def regroup(n, k):
+            src = rawt[(n, k)]
+            gt = grp.tile([P, W, 4], BF16, name="grp%d" % k, tag="grp%d" % k, align_bytes=64)
+            v = split_of(n)[k]
+            if v > 0:
+                nc.vector.tensor_copy(
+                    out=gt[:, 0:v, :].rearrange("p (c i) t -> p c t i", i=4),
+                    in_=src[:, :, 0:v].rearrange("p t (c i) -> p c t i", i=4),
+                )
+            if v < W:
+                nc.scalar.copy(
+                    out=gt[:, v:W, :].rearrange("p (c i) t -> p c t i", i=4),
+                    in_=src[:, :, v:W].rearrange("p t (c i) -> p c t i", i=4),
+                )
+            grouped[(n, k)] = gt
+
+        def quant(n, k):
+            cw = cod.tile([P, W], U32, name="cw%d" % k, tag="cw%d" % k, align_bytes=64)
+            cs = cod.tile([P, W], U8, name="cs%d" % k, tag="cs%d" % k, align_bytes=64)
+            nc.vector.quantize_mx(
+                out=cw[:].bitcast(FP8X4),
+                scales=cs[:],
+                in_=grouped[(n, k)][:].rearrange("p w j -> p (w j)"),
+            )
+            codes[(n, k)] = (cw, cs)
+
+        def first_mm(n, h):
+            xc, xsc = xcodes[n // C]
+            bcols = slice(h * P, (h + 1) * P)
+            pair = []
+            for k in range(2):
+                bank = psum.tile([P, 4, P], F32, name="ps%d" % k, tag="ps%d" % k)
+                cw, cs = codes[(n, k)]
+                for t in range(4):
+                    fcols = slice(t * P, (t + 1) * P)
+                    nc.tensor.matmul_mx(
+                        out=bank[:, t, :],
+                        lhsT=cw[:, fcols].bitcast(FP8X4),
+                        lhsT_scale=cs[:, fcols],
+                        rhs=xc[:, bcols].bitcast(FP8X4),
+                        rhs_scale=xsc[:, bcols],
+                        start=True,
+                        stop=True,
+                    )
+                pair.append(bank)
+            banks[(n, h)] = pair
+
+        def silu(n, h):
+            sl = hid.tile([P, P, 4], F32, name="sl", tag="sl", bufs=4)
+            nc.scalar.activation(out=sl[:], in_=banks[(n, h)][0][:].rearrange("p t b -> p b t"), func=SILU)
+            silus[(n, h)] = sl
+
+        def mult(n, h):
+            if h == 0:
+                hgrp[n] = hid.tile([P, H, P, 4], BF16, name="hg", tag="hg", align_bytes=64)
+            nc.vector.tensor_tensor(
+                out=hgrp[n][:, h, :, :],
+                in0=banks[(n, h)][1][:].rearrange("p t b -> p b t"),
+                in1=silus[(n, h)][:],
+                op=MULT,
+            )
+
+        def h_quant(n):
+            hc = hid.tile([P, H * P], U32, name="hc", tag="hc", align_bytes=64)
+            hs = hid.tile([P, H * P], U8, name="hs", tag="hs", align_bytes=64)
+            nc.vector.quantize_mx(
+                out=hc[:].bitcast(FP8X4),
+                scales=hs[:],
+                in_=hgrp[n][:].rearrange("p h b t -> p (h b t)"),
+            )
+            hcodes[n] = (hc, hs)
+
+        def second_mm(n):
+            g, c = divmod(n, C)
+            if c == 0:
+                obanks[g] = [psum.tile([P, O], F32, name="po", tag="po", bufs=2) for h in range(H)]
+            hc, hs = hcodes[n]
+            cw, cs = codes[(n, 2)]
+            for h in range(H):
+                bcols = slice(h * P, (h + 1) * P)
+                nc.tensor.matmul_mx(
+                    out=obanks[g][h][:],
+                    lhsT=hc[:, bcols].bitcast(FP8X4),
+                    lhsT_scale=hs[:, bcols],
+                    rhs=cw[:].bitcast(FP8X4),
+                    rhs_scale=cs[:],
+                    start=(c == 0),
+                    stop=(c == C - 1),
+                )
+
+        def finish(g, h, on_vector):
+            ot = res.tile([P, O], F32, name="ot", tag="ot")
+            if on_vector:
+                nc.vector.tensor_copy(out=ot[:], in_=obanks[g][h][:])
+            else:
+                nc.scalar.copy(out=ot[:], in_=obanks[g][h][:])
+            nc.sync.dma_start(out=ov[g, h], in_=ot[:])
+
+        warm = const.tile([P, 8], F32, name="warm", tag="warm")
+        warm2 = const.tile([P, 8], F32, name="warm2", tag="warm2")
+        nc.vector.memset(warm[:], 0.0)
+        nc.scalar.activation(out=warm2[:], in_=warm[:], func=SILU)
+        ident = const.tile([P, P], F32, name="ident", tag="ident")
+        make_identity(nc, ident[:])
+
+        load_x(0)
+        for m in range(RAW_BUFS):
+            load_round(m)
+
+        x_transposes(0)
+        x_evac(0)
+        x_quant(0)
+        regroup(0, 0)
+        regroup(0, 1)
+        load_round(RAW_BUFS)
+
+        for n in range(NSTEP + 1):
+            g, c = divmod(n, C)
+            live = n < NSTEP
+            if live:
+                quant(n, 0)
+                quant(n, 1)
+                first_mm(n, 0)
+            if n >= 1:
+                mult(n - 1, 0)
+                mult(n - 1, 1)
+            if live:
+                first_mm(n, 1)
+            if n >= 1:
+                quant(n - 1, 2)
+                h_quant(n - 1)
+                second_mm(n - 1)
+            if live and c == 3 and g + 1 < G:
+                x_quant(g + 1)
+            if live and c == 2 and g + 1 < G:
+                x_transposes(g + 1)
+            if n + 1 < NSTEP:
+                regroup(n + 1, 0)
+                regroup(n + 1, 1)
+            if live:
+                regroup(n, 2)
+                load_round(n + 1 + RAW_BUFS)
+                silu(n, 0)
+                silu(n, 1)
+            if live and c == 2 and g + 1 < G:
+                x_evac(g + 1)
+            if n >= 1 and c == 0:
+                finish(g - 1, 0, n == NSTEP)
+                finish(g - 1, 1, False)

@@ -10,6 +10,7 @@ U8 = mybir.dt.uint8
 FP8X4 = mybir.dt.float8_e4m3fn_x4
 SILU = mybir.ActivationFunctionType.Silu
 MULT = mybir.AluOpType.mult
+ADD = mybir.AluOpType.add
 
 P = 128
 G = 4
@@ -23,15 +24,20 @@ NSTEP = G * C
 
 FLOPS = 2 * 1024 * D * F * 2 + 2 * 1024 * F * O
 
-VD = 216
+VD = 96
+GP = 176
 FIRST = 336
 RAW_BUFS = 6
 
 
-def split_of(n):
+def split_of(n, k):
+    if k == 2:
+        return (VD, 0)
     if n == 0:
-        return (FIRST, FIRST, VD)
-    return (W, 0, VD)
+        return (FIRST, 0)
+    if k == 0:
+        return (W, 0)
+    return (0, GP)
 
 
 def tile_groupedmlp_plana_kernel(tc, x, gate_weight, up_weight, down_weight, out):
@@ -114,17 +120,27 @@ def tile_groupedmlp_plana_kernel(tc, x, gate_weight, up_weight, down_weight, out
 
         def regroup(n, k):
             src = rawt[(n, k)]
-            gt = grp.tile([P, W, 4], BF16, name="grp%d" % k, tag="grp%d" % k, align_bytes=64)
-            v = split_of(n)[k]
+            gt = grp.tile([P, W, 4], BF16, name="grp%d" % k, tag="grp%d" % k, bufs=(2, 1, 2)[k], align_bytes=64)
+            v, pool_cols = split_of(n, k)
+            e = W - pool_cols
+            if pool_cols > 0:
+                nc.gpsimd.tensor_scalar(
+                    out=gt[:, e:W, :],
+                    in0=src[:, :, e:W].rearrange("p t w -> p w t"),
+                    scalar1=1.0,
+                    scalar2=0.0,
+                    op0=MULT,
+                    op1=ADD,
+                )
             if v > 0:
                 nc.vector.tensor_copy(
                     out=gt[:, 0:v, :].rearrange("p (c i) t -> p c t i", i=4),
                     in_=src[:, :, 0:v].rearrange("p t (c i) -> p c t i", i=4),
                 )
-            if v < W:
+            if v < e:
                 nc.scalar.copy(
-                    out=gt[:, v:W, :].rearrange("p (c i) t -> p c t i", i=4),
-                    in_=src[:, :, v:W].rearrange("p t (c i) -> p c t i", i=4),
+                    out=gt[:, v:e, :].rearrange("p (c i) t -> p c t i", i=4),
+                    in_=src[:, :, v:e].rearrange("p t (c i) -> p c t i", i=4),
                 )
             grouped[(n, k)] = gt
 
@@ -248,11 +264,12 @@ def tile_groupedmlp_plana_kernel(tc, x, gate_weight, up_weight, down_weight, out
                 x_quant(g + 1)
             if live and c == 2 and g + 1 < G:
                 x_transposes(g + 1)
+            if live:
+                regroup(n, 2)
             if n + 1 < NSTEP:
                 regroup(n + 1, 0)
                 regroup(n + 1, 1)
             if live:
-                regroup(n, 2)
                 load_round(n + 1 + RAW_BUFS)
                 silu(n, 0)
                 silu(n, 1)

@@ -10,7 +10,6 @@ U8 = mybir.dt.uint8
 FP8X4 = mybir.dt.float8_e4m3fn_x4
 SILU = mybir.ActivationFunctionType.Silu
 MULT = mybir.AluOpType.mult
-ADD = mybir.AluOpType.add
 
 P = 128
 G = 4
@@ -24,20 +23,19 @@ NSTEP = G * C
 
 FLOPS = 2 * 1024 * D * F * 2 + 2 * 1024 * F * O
 
-VD = 96
-GP = 176
+VD = 176
+VD_END = 200
 FIRST = 336
 RAW_BUFS = 6
+LAG = 3
 
 
-def split_of(n, k):
-    if k == 2:
-        return (VD, 0)
+def split_of(n):
     if n == 0:
-        return (FIRST, 0)
-    if k == 0:
-        return (W, 0)
-    return (0, GP)
+        return (FIRST, FIRST, VD)
+    if n >= NSTEP - LAG + 1:
+        return (W, 0, VD_END)
+    return (W, 0, VD)
 
 
 def tile_groupedmlp_plana_kernel(tc, x, gate_weight, up_weight, down_weight, out):
@@ -90,8 +88,8 @@ def tile_groupedmlp_plana_kernel(tc, x, gate_weight, up_weight, down_weight, out
             if m < NSTEP:
                 load_unit(m, 0)
                 load_unit(m, 1)
-            if 1 <= m <= NSTEP:
-                load_unit(m - 1, 2)
+            if 0 <= m - LAG < NSTEP:
+                load_unit(m - LAG, 2)
             if m % C == 1 and m // C + 1 < G:
                 load_x(m // C + 1)
 
@@ -120,27 +118,17 @@ def tile_groupedmlp_plana_kernel(tc, x, gate_weight, up_weight, down_weight, out
 
         def regroup(n, k):
             src = rawt[(n, k)]
-            gt = grp.tile([P, W, 4], BF16, name="grp%d" % k, tag="grp%d" % k, bufs=(2, 1, 2)[k], align_bytes=64)
-            v, pool_cols = split_of(n, k)
-            e = W - pool_cols
-            if pool_cols > 0:
-                nc.gpsimd.tensor_scalar(
-                    out=gt[:, e:W, :],
-                    in0=src[:, :, e:W].rearrange("p t w -> p w t"),
-                    scalar1=1.0,
-                    scalar2=0.0,
-                    op0=MULT,
-                    op1=ADD,
-                )
+            gt = grp.tile([P, W, 4], BF16, name="grp%d" % k, tag="grp%d" % k, align_bytes=64)
+            v = split_of(n)[k]
             if v > 0:
                 nc.vector.tensor_copy(
                     out=gt[:, 0:v, :].rearrange("p (c i) t -> p c t i", i=4),
                     in_=src[:, :, 0:v].rearrange("p t (c i) -> p c t i", i=4),
                 )
-            if v < e:
+            if v < W:
                 nc.scalar.copy(
-                    out=gt[:, v:e, :].rearrange("p (c i) t -> p c t i", i=4),
-                    in_=src[:, :, v:e].rearrange("p t (c i) -> p c t i", i=4),
+                    out=gt[:, v:W, :].rearrange("p (c i) t -> p c t i", i=4),
+                    in_=src[:, :, v:W].rearrange("p t (c i) -> p c t i", i=4),
                 )
             grouped[(n, k)] = gt
 
@@ -191,8 +179,8 @@ def tile_groupedmlp_plana_kernel(tc, x, gate_weight, up_weight, down_weight, out
             )
 
         def h_quant(n):
-            hc = hid.tile([P, H * P], U32, name="hc", tag="hc", align_bytes=64)
-            hs = hid.tile([P, H * P], U8, name="hs", tag="hs", align_bytes=64)
+            hc = hid.tile([P, H * P], U32, name="hc", tag="hc", bufs=LAG + 2, align_bytes=64)
+            hs = hid.tile([P, H * P], U8, name="hs", tag="hs", bufs=LAG + 2, align_bytes=64)
             nc.vector.quantize_mx(
                 out=hc[:].bitcast(FP8X4),
                 scales=hs[:],
@@ -244,37 +232,40 @@ def tile_groupedmlp_plana_kernel(tc, x, gate_weight, up_weight, down_weight, out
         regroup(0, 1)
         load_round(RAW_BUFS)
 
-        for n in range(NSTEP + 1):
+        for n in range(NSTEP + LAG):
             g, c = divmod(n, C)
+            d = n - LAG
             live = n < NSTEP
             if live:
                 quant(n, 0)
                 quant(n, 1)
                 first_mm(n, 0)
-            if n >= 1:
+            if 1 <= n <= NSTEP:
                 mult(n - 1, 0)
                 mult(n - 1, 1)
             if live:
                 first_mm(n, 1)
-            if n >= 1:
-                quant(n - 1, 2)
+            if d >= 0:
+                quant(d, 2)
+            if 1 <= n <= NSTEP:
                 h_quant(n - 1)
-                second_mm(n - 1)
+            if d >= 0:
+                second_mm(d)
             if live and c == 3 and g + 1 < G:
                 x_quant(g + 1)
             if live and c == 2 and g + 1 < G:
                 x_transposes(g + 1)
-            if live:
-                regroup(n, 2)
             if n + 1 < NSTEP:
                 regroup(n + 1, 0)
                 regroup(n + 1, 1)
+            if 0 <= d + 1 < NSTEP:
+                regroup(d + 1, 2)
+            load_round(n + 1 + RAW_BUFS)
             if live:
-                load_round(n + 1 + RAW_BUFS)
                 silu(n, 0)
                 silu(n, 1)
             if live and c == 2 and g + 1 < G:
                 x_evac(g + 1)
-            if n >= 1 and c == 0:
-                finish(g - 1, 0, n == NSTEP)
-                finish(g - 1, 1, False)
+            if d >= 0 and d % C == C - 1:
+                finish(d // C, 0, d == NSTEP - 1)
+                finish(d // C, 1, False)

@@ -23,8 +23,8 @@ NSTEP = G * C
 
 FLOPS = 2 * 1024 * D * F * 2 + 2 * 1024 * F * O
 
-VD = 176
-VD_END = 200
+VD = 256
+VD_END = 256
 FIRST = 336
 RAW_BUFS = 6
 LAG = 3

@@ -10,6 +10,7 @@ U8 = mybir.dt.uint8
 FP8X4 = mybir.dt.float8_e4m3fn_x4
 SILU = mybir.ActivationFunctionType.Silu
 MULT = mybir.AluOpType.mult
+ADD = mybir.AluOpType.add
 
 P = 128
 G = 4
@@ -23,19 +24,20 @@ NSTEP = G * C
 
 FLOPS = 2 * 1024 * D * F * 2 + 2 * 1024 * F * O
 
-VD = 256
-VD_END = 256
+VD = 264
+GP = 160
 FIRST = 336
 RAW_BUFS = 6
-LAG = 3
 
 
-def split_of(n):
-    if n == 0:
-        return (FIRST, FIRST, VD)
-    if n >= NSTEP - LAG + 1:
-        return (W, 0, VD_END)
-    return (W, 0, VD)
+def split_of(n, k):
+    if k == 2:
+        return (VD, 0)
+    if n <= 1:
+        return ((FIRST, 0), (FIRST, 0)) [k] if n == 0 else ((W, 0), (0, 0))[k]
+    if k == 0:
+        return (W - GP, GP)
+    return (0, 0)
 
 
 def tile_groupedmlp_plana_kernel(tc, x, gate_weight, up_weight, down_weight, out):
@@ -88,8 +90,8 @@ def tile_groupedmlp_plana_kernel(tc, x, gate_weight, up_weight, down_weight, out
             if m < NSTEP:
                 load_unit(m, 0)
                 load_unit(m, 1)
-            if 0 <= m - LAG < NSTEP:
-                load_unit(m - LAG, 2)
+            if 1 <= m <= NSTEP:
+                load_unit(m - 1, 2)
             if m % C == 1 and m // C + 1 < G:
                 load_x(m // C + 1)
 
@@ -119,16 +121,26 @@ def tile_groupedmlp_plana_kernel(tc, x, gate_weight, up_weight, down_weight, out
         def regroup(n, k):
             src = rawt[(n, k)]
             gt = grp.tile([P, W, 4], BF16, name="grp%d" % k, tag="grp%d" % k, align_bytes=64)
-            v = split_of(n)[k]
+            v, pool_cols = split_of(n, k)
+            e = W - pool_cols
+            if pool_cols > 0:
+                nc.gpsimd.tensor_scalar(
+                    out=gt[:, e:W, :],
+                    in0=src[:, :, e:W].rearrange("p t w -> p w t"),
+                    scalar1=1.0,
+                    scalar2=0.0,
+                    op0=MULT,
+                    op1=ADD,
+                )
             if v > 0:
                 nc.vector.tensor_copy(
                     out=gt[:, 0:v, :].rearrange("p (c i) t -> p c t i", i=4),
                     in_=src[:, :, 0:v].rearrange("p t (c i) -> p c t i", i=4),
                 )
-            if v < W:
+            if v < e:
                 nc.scalar.copy(
-                    out=gt[:, v:W, :].rearrange("p (c i) t -> p c t i", i=4),
-                    in_=src[:, :, v:W].rearrange("p t (c i) -> p c t i", i=4),
+                    out=gt[:, v:e, :].rearrange("p (c i) t -> p c t i", i=4),
+                    in_=src[:, :, v:e].rearrange("p t (c i) -> p c t i", i=4),
                 )
             grouped[(n, k)] = gt
 
@@ -179,8 +191,8 @@ def tile_groupedmlp_plana_kernel(tc, x, gate_weight, up_weight, down_weight, out
             )
 
         def h_quant(n):
-            hc = hid.tile([P, H * P], U32, name="hc", tag="hc", bufs=LAG + 2, align_bytes=64)
-            hs = hid.tile([P, H * P], U8, name="hs", tag="hs", bufs=LAG + 2, align_bytes=64)
+            hc = hid.tile([P, H * P], U32, name="hc", tag="hc", align_bytes=64)
+            hs = hid.tile([P, H * P], U8, name="hs", tag="hs", align_bytes=64)
             nc.vector.quantize_mx(
                 out=hc[:].bitcast(FP8X4),
                 scales=hs[:],
@@ -232,25 +244,22 @@ def tile_groupedmlp_plana_kernel(tc, x, gate_weight, up_weight, down_weight, out
         regroup(0, 1)
         load_round(RAW_BUFS)
 
-        for n in range(NSTEP + LAG):
+        for n in range(NSTEP + 1):
             g, c = divmod(n, C)
-            d = n - LAG
             live = n < NSTEP
             if live:
                 quant(n, 0)
                 quant(n, 1)
                 first_mm(n, 0)
-            if 1 <= n <= NSTEP:
+            if n >= 1:
                 mult(n - 1, 0)
                 mult(n - 1, 1)
             if live:
                 first_mm(n, 1)
-            if d >= 0:
-                quant(d, 2)
-            if 1 <= n <= NSTEP:
+            if n >= 1:
+                quant(n - 1, 2)
                 h_quant(n - 1)
-            if d >= 0:
-                second_mm(d)
+                second_mm(n - 1)
             if live and c == 3 and g + 1 < G:
                 x_quant(g + 1)
             if live and c == 2 and g + 1 < G:
@@ -258,14 +267,13 @@ def tile_groupedmlp_plana_kernel(tc, x, gate_weight, up_weight, down_weight, out
             if n + 1 < NSTEP:
                 regroup(n + 1, 0)
                 regroup(n + 1, 1)
-            if 0 <= d + 1 < NSTEP:
-                regroup(d + 1, 2)
-            load_round(n + 1 + RAW_BUFS)
             if live:
+                regroup(n, 2)
+                load_round(n + 1 + RAW_BUFS)
                 silu(n, 0)
                 silu(n, 1)
             if live and c == 2 and g + 1 < G:
                 x_evac(g + 1)
-            if d >= 0 and d % C == C - 1:
-                finish(d // C, 0, d == NSTEP - 1)
-                finish(d // C, 1, False)
+            if n >= 1 and c == 0:
+                finish(g - 1, 0, n == NSTEP)
+                finish(g - 1, 1, False)

@@ -24,15 +24,16 @@ NSTEP = G * C
 
 FLOPS = 2 * 1024 * D * F * 2 + 2 * 1024 * F * O
 
-VD = 264
-GP = 160
+VD = 280
+VD_LAST = 128
+GP = 176
 FIRST = 336
 RAW_BUFS = 6
 
 
 def split_of(n, k):
     if k == 2:
-        return (VD, 0)
+        return (VD_LAST if n == NSTEP - 1 else VD, 0)
     if n <= 1:
         return ((FIRST, 0), (FIRST, 0)) [k] if n == 0 else ((W, 0), (0, 0))[k]
     if k == 0:

@@ -24,9 +24,9 @@ NSTEP = G * C
 
 FLOPS = 2 * 1024 * D * F * 2 + 2 * 1024 * F * O
 
-VD = 280
-VD_LAST = 128
-GP = 176
+VD = 296
+VD_LAST = 64
+GP = 208
 FIRST = 336
 RAW_BUFS = 6
 

@@ -24,16 +24,14 @@ NSTEP = G * C
 
 FLOPS = 2 * 1024 * D * F * 2 + 2 * 1024 * F * O
 
-VD = 296
-VD_LAST = 64
 GP = 208
 FIRST = 336
 RAW_BUFS = 6
+PE_COLS = 256
+VDOWN = 256
 
 
 def split_of(n, k):
-    if k == 2:
-        return (VD_LAST if n == NSTEP - 1 else VD, 0)
     if n <= 1:
         return ((FIRST, 0), (FIRST, 0)) [k] if n == 0 else ((W, 0), (0, 0))[k]
     if k == 0:
@@ -57,7 +55,7 @@ def tile_groupedmlp_plana_kernel(tc, x, gate_weight, up_weight, down_weight, out
         xs = ctx.enter_context(tc.tile_pool(name="xs", bufs=2))
         hid = ctx.enter_context(tc.tile_pool(name="hid", bufs=2))
         res = ctx.enter_context(tc.tile_pool(name="res", bufs=4))
-        psum = ctx.enter_context(tc.psum_pool(name="psum", bufs=3))
+        psum = ctx.enter_context(tc.psum_pool(name="psum", bufs=2))
         ctx.enter_context(tc.manual_schedule())
 
         rawt = {}
@@ -72,6 +70,7 @@ def tile_groupedmlp_plana_kernel(tc, x, gate_weight, up_weight, down_weight, out
         hgrp = {}
         hcodes = {}
         obanks = {}
+        pibanks = {}
 
         def load_x(g):
             xr = xs.tile([P, H, D], BF16, name="xr", tag="xr", bufs=G)
@@ -98,7 +97,7 @@ def tile_groupedmlp_plana_kernel(tc, x, gate_weight, up_weight, down_weight, out
 
         def x_transposes(g):
             words = xraw[g][:].bitcast(F32).rearrange("p h (w u) -> p h u w", u=2)
-            xt = psum.tile([P, H, 2, P], F32, name="xt", tag="ps0")
+            xt = psum.tile([P, H, 2, P], F32, name="xt", tag="ps0", bufs=2)
             for h in range(H):
                 for u in range(2):
                     nc.tensor.transpose(out=xt[:, h, u, :], in_=words[:, h, u, :], identity=ident[:])
@@ -145,6 +144,29 @@ def tile_groupedmlp_plana_kernel(tc, x, gate_weight, up_weight, down_weight, out
                 )
             grouped[(n, k)] = gt
 
+        def pe_group(n):
+            bank = psum.tile([P, PE_COLS, 4], BF16, name="pi", tag="pi", bufs=1)
+            for w in range(0, PE_COLS, P):
+                nc.tensor.matmul(
+                    out=bank[:, w : w + P, :],
+                    lhsT=ident16[:],
+                    rhs=rawt[(n, 2)][:, :, w : w + P].rearrange("p t w -> p w t"),
+                    start=True,
+                    stop=True,
+                )
+            pibanks[n] = bank
+
+        def regroup_down(n):
+            src = rawt[(n, 2)]
+            gt = grp.tile([P, W, 4], BF16, name="grp2", tag="grp2", align_bytes=64)
+            nc.scalar.copy(out=gt[:, 0:PE_COLS, :], in_=pibanks[n][:])
+            e = PE_COLS + VDOWN
+            nc.vector.tensor_copy(
+                out=gt[:, PE_COLS:e, :].rearrange("p (c i) t -> p c t i", i=4),
+                in_=src[:, :, PE_COLS:e].rearrange("p t (c i) -> p c t i", i=4),
+            )
+            grouped[(n, 2)] = gt
+
         def quant(n, k):
             cw = cod.tile([P, W], U32, name="cw%d" % k, tag="cw%d" % k, align_bytes=64)
             cs = cod.tile([P, W], U8, name="cs%d" % k, tag="cs%d" % k, align_bytes=64)
@@ -160,7 +182,7 @@ def tile_groupedmlp_plana_kernel(tc, x, gate_weight, up_weight, down_weight, out
             bcols = slice(h * P, (h + 1) * P)
             pair = []
             for k in range(2):
-                bank = psum.tile([P, 4, P], F32, name="ps%d" % k, tag="ps%d" % k)
+                bank = psum.tile([P, 4, P], F32, name="ps%d" % k, tag="ps%d" % k, bufs=2 + k)
                 cw, cs = codes[(n, k)]
                 for t in range(4):
                     fcols = slice(t * P, (t + 1) * P)
@@ -233,6 +255,8 @@ def tile_groupedmlp_plana_kernel(tc, x, gate_weight, up_weight, down_weight, out
         nc.scalar.activation(out=warm2[:], in_=warm[:], func=SILU)
         ident = const.tile([P, P], F32, name="ident", tag="ident")
         make_identity(nc, ident[:])
+        ident16 = const.tile([P, P], BF16, name="ident16", tag="ident16")
+        make_identity(nc, ident16[:])
 
         load_x(0)
         for m in range(RAW_BUFS):
@@ -252,6 +276,7 @@ def tile_groupedmlp_plana_kernel(tc, x, gate_weight, up_weight, down_weight, out
                 quant(n, 0)
                 quant(n, 1)
                 first_mm(n, 0)
+                pe_group(n)
             if n >= 1:
                 mult(n - 1, 0)
                 mult(n - 1, 1)
@@ -269,7 +294,7 @@ def tile_groupedmlp_plana_kernel(tc, x, gate_weight, up_weight, down_weight, out
                 regroup(n + 1, 0)
                 regroup(n + 1, 1)
             if live:
-                regroup(n, 2)
+                regroup_down(n)
                 load_round(n + 1 + RAW_BUFS)
                 silu(n, 0)
                 silu(n, 1)

@@ -148,9 +148,9 @@ def tile_groupedmlp_plana_kernel(tc, x, gate_weight, up_weight, down_weight, out
             bank = psum.tile([P, PE_COLS, 4], BF16, name="pi", tag="pi", bufs=1)
             for w in range(0, PE_COLS, P):
                 nc.tensor.matmul(
-                    out=bank[:, w : w + P, :],
+                    out=bank[:, w : w + P, :].rearrange("p (c i) t -> p c t i", i=4),
                     lhsT=ident16[:],
-                    rhs=rawt[(n, 2)][:, :, w : w + P].rearrange("p t w -> p w t"),
+                    rhs=rawt[(n, 2)][:, :, w : w + P].rearrange("p t (c i) -> p c t i", i=4),
                     start=True,
                     stop=True,
                 )

@@ -24,19 +24,36 @@ NSTEP = G * C
 
 FLOPS = 2 * 1024 * D * F * 2 + 2 * 1024 * F * O
 
-GP = 208
-FIRST = 336
 RAW_BUFS = 6
+GP = 208
 PE_COLS = 256
-VDOWN = 256
+VG0 = 512
+SG = 0
+SD = 32
+VE0 = 272
+VE1 = 256
+VE2 = 192
+LG = 0
+LSU = 0
+LSD = 0
 
 
-def split_of(n, k):
-    if n <= 1:
-        return ((FIRST, 0), (FIRST, 0)) [k] if n == 0 else ((W, 0), (0, 0))[k]
-    if k == 0:
-        return (W - GP, GP)
-    return (0, 0)
+def shares(n, k):
+    if n == 0 and k < 2:
+        return ((0, VG0, W - VG0, 0), (0, VE0, W - VE0, 0))[k]
+    if n == 1 and k < 2:
+        return (0, VE1, W - VE1, 0)
+    if k == 2:
+        if n == NSTEP - 1:
+            return (PE_COLS, LSD, W - PE_COLS - LG - LSD, LG)
+        if n == 0:
+            return (0, VE2, W - VE2, 0)
+        return (PE_COLS, W - PE_COLS - SD, SD, 0)
+    if k == 1:
+        if n == NSTEP - 1:
+            return (0, LSU, W - LG - LSU, LG)
+        return (0, 0, W, 0)
+    return (0, W - GP - SG, SG, GP)
 
 
 def tile_groupedmlp_plana_kernel(tc, x, gate_weight, up_weight, down_weight, out):
@@ -90,8 +107,7 @@ def tile_groupedmlp_plana_kernel(tc, x, gate_weight, up_weight, down_weight, out
             if m < NSTEP:
                 load_unit(m, 0)
                 load_unit(m, 1)
-            if 1 <= m <= NSTEP:
-                load_unit(m - 1, 2)
+                load_unit(m, 2)
             if m % C == 1 and m // C + 1 < G:
                 load_x(m // C + 1)
 
@@ -118,54 +134,50 @@ def tile_groupedmlp_plana_kernel(tc, x, gate_weight, up_weight, down_weight, out
             )
             xcodes[g] = (xc, xsc)
 
+        def regroup_pe(n, k):
+            cols = shares(n, k)[0]
+            if cols == 0:
+                return
+            bank = psum.tile([P, PE_COLS, 4], BF16, name="pi", tag="pi", bufs=1)
+            for w in range(0, PE_COLS, P):
+                nc.tensor.matmul(
+                    out=bank[:, w : w + P, :],
+                    lhsT=ident16[:],
+                    rhs=rawt[(n, k)][:, :, w : w + P].rearrange("p t w -> p w t"),
+                    start=True,
+                    stop=True,
+                )
+            pibanks[(n, k)] = bank
+
         def regroup(n, k):
             src = rawt[(n, k)]
             gt = grp.tile([P, W, 4], BF16, name="grp%d" % k, tag="grp%d" % k, align_bytes=64)
-            v, pool_cols = split_of(n, k)
-            e = W - pool_cols
-            if pool_cols > 0:
+            t_cols, v_cols, s_cols, g_cols = shares(n, k)
+            v0 = t_cols
+            s0 = v0 + v_cols
+            g0 = s0 + s_cols
+            if g_cols > 0:
                 nc.gpsimd.tensor_scalar(
-                    out=gt[:, e:W, :],
-                    in0=src[:, :, e:W].rearrange("p t w -> p w t"),
+                    out=gt[:, g0:W, :],
+                    in0=src[:, :, g0:W].rearrange("p t w -> p w t"),
                     scalar1=1.0,
                     scalar2=0.0,
                     op0=MULT,
                     op1=ADD,
                 )
-            if v > 0:
+            if t_cols > 0:
+                nc.scalar.copy(out=gt[:, 0:t_cols, :], in_=pibanks[(n, k)][:])
+            if v_cols > 0:
                 nc.vector.tensor_copy(
-                    out=gt[:, 0:v, :].rearrange("p (c i) t -> p c t i", i=4),
-                    in_=src[:, :, 0:v].rearrange("p t (c i) -> p c t i", i=4),
+                    out=gt[:, v0:s0, :].rearrange("p (c i) t -> p c t i", i=4),
+                    in_=src[:, :, v0:s0].rearrange("p t (c i) -> p c t i", i=4),
                 )
-            if v < e:
+            if s_cols > 0:
                 nc.scalar.copy(
-                    out=gt[:, v:e, :].rearrange("p (c i) t -> p c t i", i=4),
-                    in_=src[:, :, v:e].rearrange("p t (c i) -> p c t i", i=4),
+                    out=gt[:, s0:g0, :].rearrange("p (c i) t -> p c t i", i=4),
+                    in_=src[:, :, s0:g0].rearrange("p t (c i) -> p c t i", i=4),
                 )
             grouped[(n, k)] = gt
-
-        def pe_group(n):
-            bank = psum.tile([P, PE_COLS, 4], BF16, name="pi", tag="pi", bufs=1)
-            for w in range(0, PE_COLS, P):
-                nc.tensor.matmul(
-                    out=bank[:, w : w + P, :].rearrange("p (c i) t -> p c t i", i=4),
-                    lhsT=ident16[:],
-                    rhs=rawt[(n, 2)][:, :, w : w + P].rearrange("p t (c i) -> p c t i", i=4),
-                    start=True,
-                    stop=True,
-                )
-            pibanks[n] = bank
-
-        def regroup_down(n):
-            src = rawt[(n, 2)]
-            gt = grp.tile([P, W, 4], BF16, name="grp2", tag="grp2", align_bytes=64)
-            nc.scalar.copy(out=gt[:, 0:PE_COLS, :], in_=pibanks[n][:])
-            e = PE_COLS + VDOWN
-            nc.vector.tensor_copy(
-                out=gt[:, PE_COLS:e, :].rearrange("p (c i) t -> p c t i", i=4),
-                in_=src[:, :, PE_COLS:e].rearrange("p t (c i) -> p c t i", i=4),
-            )
-            grouped[(n, 2)] = gt
 
         def quant(n, k):
             cw = cod.tile([P, W], U32, name="cw%d" % k, tag="cw%d" % k, align_bytes=64)
@@ -213,23 +225,26 @@ def tile_groupedmlp_plana_kernel(tc, x, gate_weight, up_weight, down_weight, out
                 op=MULT,
             )
 
-        def h_quant(n):
-            hc = hid.tile([P, H * P], U32, name="hc", tag="hc", align_bytes=64)
-            hs = hid.tile([P, H * P], U8, name="hs", tag="hs", align_bytes=64)
+        def h_quant(n, halves):
+            if n not in hcodes:
+                hc = hid.tile([P, H * P], U32, name="hc", tag="hc", align_bytes=64)
+                hs = hid.tile([P, H * P], U8, name="hs", tag="hs", align_bytes=64)
+                hcodes[n] = (hc, hs)
+            hc, hs = hcodes[n]
+            bcols = slice(halves[0] * P, (halves[-1] + 1) * P)
             nc.vector.quantize_mx(
-                out=hc[:].bitcast(FP8X4),
-                scales=hs[:],
-                in_=hgrp[n][:].rearrange("p h b t -> p (h b t)"),
+                out=hc[:, bcols].bitcast(FP8X4),
+                scales=hs[:, bcols],
+                in_=hgrp[n][:].rearrange("p h b t -> p (h b) t")[:, bcols, :].rearrange("p b t -> p (b t)"),
             )
-            hcodes[n] = (hc, hs)
 
-        def second_mm(n):
+        def second_mm(n, halves):
             g, c = divmod(n, C)
             if c == 0:
                 obanks[g] = [psum.tile([P, O], F32, name="po", tag="po", bufs=2) for h in range(H)]
             hc, hs = hcodes[n]
             cw, cs = codes[(n, 2)]
-            for h in range(H):
+            for h in halves:
                 bcols = slice(h * P, (h + 1) * P)
                 nc.tensor.matmul_mx(
                     out=obanks[g][h][:],
@@ -258,48 +273,62 @@ def tile_groupedmlp_plana_kernel(tc, x, gate_weight, up_weight, down_weight, out
         ident16 = const.tile([P, P], BF16, name="ident16", tag="ident16")
         make_identity(nc, ident16[:])
 
+        load_unit(0, 0)
         load_x(0)
-        for m in range(RAW_BUFS):
+        load_unit(0, 1)
+        load_unit(0, 2)
+        for m in range(1, RAW_BUFS):
             load_round(m)
 
+        regroup(0, 0)
         x_transposes(0)
         x_evac(0)
+        quant(0, 0)
         x_quant(0)
-        regroup(0, 0)
         regroup(0, 1)
         load_round(RAW_BUFS)
+        regroup(0, 2)
 
         for n in range(NSTEP + 1):
             g, c = divmod(n, C)
             live = n < NSTEP
+            if n >= 1:
+                silu(n - 1, 0)
+                silu(n - 1, 1)
+            if live and c == 3 and g + 1 < G:
+                x_evac(g + 1)
+            if live and n >= 1:
+                regroup(n, 2)
+            if live and n > 1 and c == 1:
+                finish(g - 1, 0, False)
+                finish(g - 1, 1, False)
             if live:
-                quant(n, 0)
+                if n >= 1:
+                    quant(n, 0)
                 quant(n, 1)
                 first_mm(n, 0)
-                pe_group(n)
-            if n >= 1:
-                mult(n - 1, 0)
-                mult(n - 1, 1)
-            if live:
                 first_mm(n, 1)
-            if n >= 1:
-                quant(n - 1, 2)
-                h_quant(n - 1)
-                second_mm(n - 1)
-            if live and c == 3 and g + 1 < G:
-                x_quant(g + 1)
-            if live and c == 2 and g + 1 < G:
-                x_transposes(g + 1)
-            if n + 1 < NSTEP:
-                regroup(n + 1, 0)
-                regroup(n + 1, 1)
-            if live:
-                regroup_down(n)
+                if n + 1 < NSTEP:
+                    regroup_pe(n + 1, 2)
+                if n >= 1:
+                    mult(n - 1, 0)
+                    mult(n - 1, 1)
+                if n + 1 < NSTEP:
+                    regroup(n + 1, 0)
+                    regroup(n + 1, 1)
+                if n >= 1:
+                    quant(n - 1, 2)
+                    h_quant(n - 1, (0, 1))
+                    second_mm(n - 1, (0, 1))
+                if c == 3 and g + 1 < G:
+                    x_quant(g + 1)
+                if c == 2 and g + 1 < G:
+                    x_transposes(g + 1)
                 load_round(n + 1 + RAW_BUFS)
-                silu(n, 0)
-                silu(n, 1)
-            if live and c == 2 and g + 1 < G:
-                x_evac(g + 1)
-            if n >= 1 and c == 0:
-                finish(g - 1, 0, n == NSTEP)
-                finish(g - 1, 1, False)
+            else:
+                quant(n - 1, 2)
+                for h in range(H):
+                    mult(n - 1, h)
+                    h_quant(n - 1, (h,))
+                    second_mm(n - 1, (h,))
+                    finish(G - 1, h, h == 1)

@@ -25,11 +25,11 @@ NSTEP = G * C
 FLOPS = 2 * 1024 * D * F * 2 + 2 * 1024 * F * O
 
 RAW_BUFS = 6
-GP = 208
+GP = 192
 PE_COLS = 256
-VG0 = 512
+VG0 = 384
 SG = 0
-SD = 32
+SD = 0
 VE0 = 272
 VE1 = 256
 VE2 = 192
@@ -141,9 +141,9 @@ def tile_groupedmlp_plana_kernel(tc, x, gate_weight, up_weight, down_weight, out
             bank = psum.tile([P, PE_COLS, 4], BF16, name="pi", tag="pi", bufs=1)
             for w in range(0, PE_COLS, P):
                 nc.tensor.matmul(
-                    out=bank[:, w : w + P, :],
+                    out=bank[:, w : w + P, :].rearrange("p (c i) t -> p c t i", i=4),
                     lhsT=ident16[:],
-                    rhs=rawt[(n, k)][:, :, w : w + P].rearrange("p t w -> p w t"),
+                    rhs=rawt[(n, k)][:, :, w : w + P].rearrange("p t (c i) -> p c t i", i=4),
                     start=True,
                     stop=True,
                 )
@@ -274,18 +274,19 @@ def tile_groupedmlp_plana_kernel(tc, x, gate_weight, up_weight, down_weight, out
         make_identity(nc, ident16[:])
 
         load_unit(0, 0)
-        load_x(0)
         load_unit(0, 1)
+        load_x(0)
         load_unit(0, 2)
         for m in range(1, RAW_BUFS):
             load_round(m)
 
         regroup(0, 0)
         x_transposes(0)
-        x_evac(0)
         quant(0, 0)
-        x_quant(0)
         regroup(0, 1)
+        x_evac(0)
+        quant(0, 1)
+        x_quant(0)
         load_round(RAW_BUFS)
         regroup(0, 2)
 
@@ -305,7 +306,7 @@ def tile_groupedmlp_plana_kernel(tc, x, gate_weight, up_weight, down_weight, out
             if live:
                 if n >= 1:
                     quant(n, 0)
-                quant(n, 1)
+                    quant(n, 1)
                 first_mm(n, 0)
                 first_mm(n, 1)
                 if n + 1 < NSTEP:

@@ -25,6 +25,7 @@ NSTEP = G * C
 FLOPS = 2 * 1024 * D * F * 2 + 2 * 1024 * F * O
 
 RAW_BUFS = 6
+PAD = 32
 GP = 192
 PE_COLS = 256
 VG0 = 384
@@ -96,11 +97,12 @@ def tile_groupedmlp_plana_kernel(tc, x, gate_weight, up_weight, down_weight, out
 
         def load_unit(n, k):
             g, c = divmod(n, C)
-            rt = raw.tile([P, 4, W], BF16, name="raw%d" % k, tag="raw%d" % k)
+            padded = raw.tile([P, 4, W + PAD], BF16, name="raw%d" % k, tag="raw%d" % k)
+            rt = padded[:, :, 0:W]
             if k == 2:
-                nc.sync.dma_start(out=rt[:], in_=dv[g, c])
+                nc.sync.dma_start(out=rt, in_=dv[g, c])
             else:
-                nc.sync.dma_start(out=rt[:], in_=(gv, uv)[k][g, :, :, c * W : (c + 1) * W])
+                nc.sync.dma_start(out=rt, in_=(gv, uv)[k][g, :, :, c * W : (c + 1) * W])
             rawt[(n, k)] = rt
 
         def load_round(m):
@@ -113,7 +115,7 @@ def tile_groupedmlp_plana_kernel(tc, x, gate_weight, up_weight, down_weight, out
 
         def x_transposes(g):
             words = xraw[g][:].bitcast(F32).rearrange("p h (w u) -> p h u w", u=2)
-            xt = psum.tile([P, H, 2, P], F32, name="xt", tag="ps0", bufs=2)
+            xt = psum.tile([P, H, 2, P], F32, name="xt", tag="ps1", bufs=3)
             for h in range(H):
                 for u in range(2):
                     nc.tensor.transpose(out=xt[:, h, u, :], in_=words[:, h, u, :], identity=ident[:])
@@ -311,6 +313,8 @@ def tile_groupedmlp_plana_kernel(tc, x, gate_weight, up_weight, down_weight, out
                 first_mm(n, 1)
                 if n + 1 < NSTEP:
                     regroup_pe(n + 1, 2)
+                if c == 2 and g + 1 < G:
+                    x_transposes(g + 1)
                 if n >= 1:
                     mult(n - 1, 0)
                     mult(n - 1, 1)
@@ -323,8 +327,6 @@ def tile_groupedmlp_plana_kernel(tc, x, gate_weight, up_weight, down_weight, out
                     second_mm(n - 1, (0, 1))
                 if c == 3 and g + 1 < G:
                     x_quant(g + 1)
-                if c == 2 and g + 1 < G:
-                    x_transposes(g + 1)
                 load_round(n + 1 + RAW_BUFS)
             else:
                 quant(n - 1, 2)

@@ -171,8 +171,8 @@ def tile_groupedmlp_plana_kernel(tc, x, gate_weight, up_weight, down_weight, out
                 nc.scalar.copy(out=gt[:, 0:t_cols, :], in_=pibanks[(n, k)][:])
             if v_cols > 0:
                 nc.vector.tensor_copy(
-                    out=gt[:, v0:s0, :].rearrange("p (c i) t -> p c t i", i=4),
-                    in_=src[:, :, v0:s0].rearrange("p t (c i) -> p c t i", i=4),
+                    out=gt[:, v0:s0, :].rearrange("p (c i) t -> p c t i", i=8),
+                    in_=src[:, :, v0:s0].rearrange("p t (c i) -> p c t i", i=8),
                 )
             if s_cols > 0:
                 nc.scalar.copy(

@@ -176,8 +176,8 @@ def tile_groupedmlp_plana_kernel(tc, x, gate_weight, up_weight, down_weight, out
                 )
             if s_cols > 0:
                 nc.scalar.copy(
-                    out=gt[:, s0:g0, :].rearrange("p (c i) t -> p c t i", i=4),
-                    in_=src[:, :, s0:g0].rearrange("p t (c i) -> p c t i", i=4),
+                    out=gt[:, s0:g0, :].rearrange("p (c i) t -> p c t i", i=8),
+                    in_=src[:, :, s0:g0].rearrange("p t (c i) -> p c t i", i=8),
                 )
             grouped[(n, k)] = gt
 
@@ -258,13 +258,16 @@ def tile_groupedmlp_plana_kernel(tc, x, gate_weight, up_weight, down_weight, out
                     stop=(c == C - 1),
                 )
 
-        def finish(g, h, on_vector):
+        def finish(g, h):
             ot = res.tile([P, O], F32, name="ot", tag="ot")
-            if on_vector:
-                nc.vector.tensor_copy(out=ot[:], in_=obanks[g][h][:])
-            else:
-                nc.scalar.copy(out=ot[:], in_=obanks[g][h][:])
+            nc.scalar.copy(out=ot[:], in_=obanks[g][h][:])
             nc.sync.dma_start(out=ov[g, h], in_=ot[:])
+
+        def finish_in_halves(g, h):
+            for a in range(0, O, O // 2):
+                ot = res.tile([P, O // 2], F32, name="oh", tag="oh", bufs=2)
+                nc.vector.tensor_copy(out=ot[:], in_=obanks[g][h][:, a : a + O // 2])
+                nc.sync.dma_start(out=ov[g, h][:, a : a + O // 2], in_=ot[:])
 
         warm = const.tile([P, 8], F32, name="warm", tag="warm")
         warm2 = const.tile([P, 8], F32, name="warm2", tag="warm2")
@@ -303,8 +306,8 @@ def tile_groupedmlp_plana_kernel(tc, x, gate_weight, up_weight, down_weight, out
             if live and n >= 1:
                 regroup(n, 2)
             if live and n > 1 and c == 1:
-                finish(g - 1, 0, False)
-                finish(g - 1, 1, False)
+                finish(g - 1, 0)
+                finish(g - 1, 1)
             if live:
                 if n >= 1:
                     quant(n, 0)
@@ -334,4 +337,5 @@ def tile_groupedmlp_plana_kernel(tc, x, gate_weight, up_weight, down_weight, out
                     mult(n - 1, h)
                     h_quant(n - 1, (h,))
                     second_mm(n - 1, (h,))
-                    finish(G - 1, h, h == 1)
+                finish(G - 1, 0)
+                finish_in_halves(G - 1, 1)

@@ -26,7 +26,7 @@ FLOPS = 2 * 1024 * D * F * 2 + 2 * 1024 * F * O
 
 RAW_BUFS = 6
 PAD = 32
-GP = 192
+GP = 208
 PE_COLS = 256
 VG0 = 384
 SG = 0
@@ -160,15 +160,18 @@ def tile_groupedmlp_plana_kernel(tc, x, gate_weight, up_weight, down_weight, out
             g0 = s0 + s_cols
             if g_cols > 0:
                 nc.gpsimd.tensor_scalar(
-                    out=gt[:, g0:W, :],
-                    in0=src[:, :, g0:W].rearrange("p t w -> p w t"),
+                    out=gt[:, g0:W, :].rearrange("p (c i) t -> p c t i", i=8),
+                    in0=src[:, :, g0:W].rearrange("p t (c i) -> p c t i", i=8),
                     scalar1=1.0,
                     scalar2=0.0,
                     op0=MULT,
                     op1=ADD,
                 )
             if t_cols > 0:
-                nc.scalar.copy(out=gt[:, 0:t_cols, :], in_=pibanks[(n, k)][:])
+                nc.scalar.copy(
+                    out=gt[:, 0:t_cols, :].rearrange("p w t -> p (w t)"),
+                    in_=pibanks[(n, k)][:].rearrange("p w t -> p (w t)"),
+                )
             if v_cols > 0:
                 nc.vector.tensor_copy(
                     out=gt[:, v0:s0, :].rearrange("p (c i) t -> p c t i", i=8),

from contextlib import ExitStack

import concourse.mybir as mybir
from concourse.masks import make_identity

BF16 = mybir.dt.bfloat16
F32 = mybir.dt.float32
U32 = mybir.dt.uint32
U8 = mybir.dt.uint8
FP8X4 = mybir.dt.float8_e4m3fn_x4
SILU = mybir.ActivationFunctionType.Silu
MULT = mybir.AluOpType.mult
ADD = mybir.AluOpType.add

P = 128
G = 4
H = 2
D = 512
F = 2048
O = 512
C = 4
W = 512
NSTEP = G * C

FLOPS = 2 * 1024 * D * F * 2 + 2 * 1024 * F * O

RAW_BUFS = 6
PAD = 32
GP = 208
PE_COLS = 256
VG0 = 384
SG = 0
SD = 0
VE0 = 272
VE1 = 256
VE2 = 192
LG = 0
LSU = 0
LSD = 0


def shares(n, k):
    if n == 0 and k < 2:
        return ((0, VG0, W - VG0, 0), (0, VE0, W - VE0, 0))[k]
    if n == 1 and k < 2:
        return (0, VE1, W - VE1, 0)
    if k == 2:
        if n == NSTEP - 1:
            return (PE_COLS, LSD, W - PE_COLS - LG - LSD, LG)
        if n == 0:
            return (0, VE2, W - VE2, 0)
        return (PE_COLS, W - PE_COLS - SD, SD, 0)
    if k == 1:
        if n == NSTEP - 1:
            return (0, LSU, W - LG - LSU, LG)
        return (0, 0, W, 0)
    return (0, W - GP - SG, SG, GP)


def tile_groupedmlp_plana_kernel(tc, x, gate_weight, up_weight, down_weight, out):
    nc = tc.nc
    xv = x.rearrange("(h b g) d -> g b h d", h=H, g=G)
    gv = gate_weight.rearrange("g (p j) f -> g p j f", j=4)
    uv = up_weight.rearrange("g (p j) f -> g p j f", j=4)
    dv = down_weight.rearrange("g (c t p) o -> g c p t o", c=C, t=4)
    ov = out.rearrange("(h b g) o -> g h b o", h=H, g=G)

    with ExitStack() as ctx:
        const = ctx.enter_context(tc.tile_pool(name="const", bufs=1))
        raw = ctx.enter_context(tc.tile_pool(name="raw", bufs=RAW_BUFS))
        grp = ctx.enter_context(tc.tile_pool(name="grp", bufs=2))
        cod = ctx.enter_context(tc.tile_pool(name="cod", bufs=3))
        xs = ctx.enter_context(tc.tile_pool(name="xs", bufs=2))
        hid = ctx.enter_context(tc.tile_pool(name="hid", bufs=2))
        res = ctx.enter_context(tc.tile_pool(name="res", bufs=4))
        psum = ctx.enter_context(tc.psum_pool(name="psum", bufs=2))
        ctx.enter_context(tc.manual_schedule())

        rawt = {}
        xraw = {}
        xbank = {}
        xgrp = {}
        xcodes = {}
        grouped = {}
        codes = {}
        banks = {}
        silus = {}
        hgrp = {}
        hcodes = {}
        obanks = {}
        pibanks = {}

        def load_x(g):
            xr = xs.tile([P, H, D], BF16, name="xr", tag="xr", bufs=G)
            nc.sync.dma_start(out=xr[:], in_=xv[g])
            xraw[g] = xr

        def load_unit(n, k):
            g, c = divmod(n, C)
            padded = raw.tile([P, 4, W + PAD], BF16, name="raw%d" % k, tag="raw%d" % k)
            rt = padded[:, :, 0:W]
            if k == 2:
                nc.sync.dma_start(out=rt, in_=dv[g, c])
            else:
                nc.sync.dma_start(out=rt, in_=(gv, uv)[k][g, :, :, c * W : (c + 1) * W])
            rawt[(n, k)] = rt

        def load_round(m):
            if m < NSTEP:
                load_unit(m, 0)
                load_unit(m, 1)
                load_unit(m, 2)
            if m % C == 1 and m // C + 1 < G:
                load_x(m // C + 1)

        def x_transposes(g):
            words = xraw[g][:].bitcast(F32).rearrange("p h (w u) -> p h u w", u=2)
            xt = psum.tile([P, H, 2, P], F32, name="xt", tag="ps1", bufs=3)
            for h in range(H):
                for u in range(2):
                    nc.tensor.transpose(out=xt[:, h, u, :], in_=words[:, h, u, :], identity=ident[:])
            xbank[g] = xt

        def x_evac(g):
            xg = xs.tile([P, H, P, 4], BF16, name="xg", tag="xg", align_bytes=64)
            nc.scalar.copy(out=xg[:].bitcast(F32), in_=xbank[g][:].rearrange("p h u b -> p h b u"))
            xgrp[g] = xg

        def x_quant(g):
            xc = xs.tile([P, H * P], U32, name="xc", tag="xc", align_bytes=64)
            xsc = xs.tile([P, H * P], U8, name="xsc", tag="xsc", align_bytes=64)
            nc.vector.quantize_mx(
                out=xc[:].bitcast(FP8X4),
                scales=xsc[:],
                in_=xgrp[g][:].rearrange("p h b t -> p (h b t)"),
            )
            xcodes[g] = (xc, xsc)

        def regroup_pe(n, k):
            cols = shares(n, k)[0]
            if cols == 0:
                return
            bank = psum.tile([P, PE_COLS, 4], BF16, name="pi", tag="pi", bufs=1)
            for w in range(0, PE_COLS, P):
                nc.tensor.matmul(
                    out=bank[:, w : w + P, :].rearrange("p (c i) t -> p c t i", i=4),
                    lhsT=ident16[:],
                    rhs=rawt[(n, k)][:, :, w : w + P].rearrange("p t (c i) -> p c t i", i=4),
                    start=True,
                    stop=True,
                )
            pibanks[(n, k)] = bank

        def regroup(n, k):
            src = rawt[(n, k)]
            gt = grp.tile([P, W, 4], BF16, name="grp%d" % k, tag="grp%d" % k, align_bytes=64)
            t_cols, v_cols, s_cols, g_cols = shares(n, k)
            v0 = t_cols
            s0 = v0 + v_cols
            g0 = s0 + s_cols
            if g_cols > 0:
                nc.gpsimd.tensor_scalar(
                    out=gt[:, g0:W, :].rearrange("p (c i) t -> p c t i", i=8),
                    in0=src[:, :, g0:W].rearrange("p t (c i) -> p c t i", i=8),
                    scalar1=1.0,
                    scalar2=0.0,
                    op0=MULT,
                    op1=ADD,
                )
            if t_cols > 0:
                nc.scalar.copy(
                    out=gt[:, 0:t_cols, :].rearrange("p w t -> p (w t)"),
                    in_=pibanks[(n, k)][:].rearrange("p w t -> p (w t)"),
                )
            if v_cols > 0:
                nc.vector.tensor_copy(
                    out=gt[:, v0:s0, :].rearrange("p (c i) t -> p c t i", i=8),
                    in_=src[:, :, v0:s0].rearrange("p t (c i) -> p c t i", i=8),
                )
            if s_cols > 0:
                nc.scalar.copy(
                    out=gt[:, s0:g0, :].rearrange("p (c i) t -> p c t i", i=8),
                    in_=src[:, :, s0:g0].rearrange("p t (c i) -> p c t i", i=8),
                )
            grouped[(n, k)] = gt

        def quant(n, k):
            cw = cod.tile([P, W], U32, name="cw%d" % k, tag="cw%d" % k, align_bytes=64)
            cs = cod.tile([P, W], U8, name="cs%d" % k, tag="cs%d" % k, align_bytes=64)
            nc.vector.quantize_mx(
                out=cw[:].bitcast(FP8X4),
                scales=cs[:],
                in_=grouped[(n, k)][:].rearrange("p w j -> p (w j)"),
            )
            codes[(n, k)] = (cw, cs)

        def first_mm(n, h):
            xc, xsc = xcodes[n // C]
            bcols = slice(h * P, (h + 1) * P)
            pair = []
            for k in range(2):
                bank = psum.tile([P, 4, P], F32, name="ps%d" % k, tag="ps%d" % k, bufs=2 + k)
                cw, cs = codes[(n, k)]
                for t in range(4):
                    fcols = slice(t * P, (t + 1) * P)
                    nc.tensor.matmul_mx(
                        out=bank[:, t, :],
                        lhsT=cw[:, fcols].bitcast(FP8X4),
                        lhsT_scale=cs[:, fcols],
                        rhs=xc[:, bcols].bitcast(FP8X4),
                        rhs_scale=xsc[:, bcols],
                        start=True,
                        stop=True,
                    )
                pair.append(bank)
            banks[(n, h)] = pair

        def silu(n, h):
            sl = hid.tile([P, P, 4], F32, name="sl", tag="sl", bufs=4)
            nc.scalar.activation(out=sl[:], in_=banks[(n, h)][0][:].rearrange("p t b -> p b t"), func=SILU)
            silus[(n, h)] = sl

        def mult(n, h):
            if h == 0:
                hgrp[n] = hid.tile([P, H, P, 4], BF16, name="hg", tag="hg", align_bytes=64)
            nc.vector.tensor_tensor(
                out=hgrp[n][:, h, :, :],
                in0=banks[(n, h)][1][:].rearrange("p t b -> p b t"),
                in1=silus[(n, h)][:],
                op=MULT,
            )

        def h_quant(n, halves):
            if n not in hcodes:
                hc = hid.tile([P, H * P], U32, name="hc", tag="hc", align_bytes=64)
                hs = hid.tile([P, H * P], U8, name="hs", tag="hs", align_bytes=64)
                hcodes[n] = (hc, hs)
            hc, hs = hcodes[n]
            bcols = slice(halves[0] * P, (halves[-1] + 1) * P)
            nc.vector.quantize_mx(
                out=hc[:, bcols].bitcast(FP8X4),
                scales=hs[:, bcols],
                in_=hgrp[n][:].rearrange("p h b t -> p (h b) t")[:, bcols, :].rearrange("p b t -> p (b t)"),
            )

        def second_mm(n, halves):
            g, c = divmod(n, C)
            if c == 0:
                obanks[g] = [psum.tile([P, O], F32, name="po", tag="po", bufs=2) for h in range(H)]
            hc, hs = hcodes[n]
            cw, cs = codes[(n, 2)]
            for h in halves:
                bcols = slice(h * P, (h + 1) * P)
                nc.tensor.matmul_mx(
                    out=obanks[g][h][:],
                    lhsT=hc[:, bcols].bitcast(FP8X4),
                    lhsT_scale=hs[:, bcols],
                    rhs=cw[:].bitcast(FP8X4),
                    rhs_scale=cs[:],
                    start=(c == 0),
                    stop=(c == C - 1),
                )

        def finish(g, h):
            ot = res.tile([P, O], F32, name="ot", tag="ot")
            nc.scalar.copy(out=ot[:], in_=obanks[g][h][:])
            nc.sync.dma_start(out=ov[g, h], in_=ot[:])

        def finish_in_halves(g, h):
            for a in range(0, O, O // 2):
                ot = res.tile([P, O // 2], F32, name="oh", tag="oh", bufs=2)
                nc.vector.tensor_copy(out=ot[:], in_=obanks[g][h][:, a : a + O // 2])
                nc.sync.dma_start(out=ov[g, h][:, a : a + O // 2], in_=ot[:])

        warm = const.tile([P, 8], F32, name="warm", tag="warm")
        warm2 = const.tile([P, 8], F32, name="warm2", tag="warm2")
        nc.vector.memset(warm[:], 0.0)
        nc.scalar.activation(out=warm2[:], in_=warm[:], func=SILU)
        ident = const.tile([P, P], F32, name="ident", tag="ident")
        make_identity(nc, ident[:])
        ident16 = const.tile([P, P], BF16, name="ident16", tag="ident16")
        make_identity(nc, ident16[:])

        load_unit(0, 0)
        load_unit(0, 1)
        load_x(0)
        load_unit(0, 2)
        for m in range(1, RAW_BUFS):
            load_round(m)

        regroup(0, 0)
        x_transposes(0)
        quant(0, 0)
        regroup(0, 1)
        x_evac(0)
        quant(0, 1)
        x_quant(0)
        load_round(RAW_BUFS)
        regroup(0, 2)

        for n in range(NSTEP + 1):
            g, c = divmod(n, C)
            live = n < NSTEP
            if n >= 1:
                silu(n - 1, 0)
                silu(n - 1, 1)
            if live and c == 3 and g + 1 < G:
                x_evac(g + 1)
            if live and n >= 1:
                regroup(n, 2)
            if live and n > 1 and c == 1:
                finish(g - 1, 0)
                finish(g - 1, 1)
            if live:
                if n >= 1:
                    quant(n, 0)
                    quant(n, 1)
                first_mm(n, 0)
                first_mm(n, 1)
                if n + 1 < NSTEP:
                    regroup_pe(n + 1, 2)
                if c == 2 and g + 1 < G:
                    x_transposes(g + 1)
                if n >= 1:
                    mult(n - 1, 0)
                    mult(n - 1, 1)
                if n + 1 < NSTEP:
                    regroup(n + 1, 0)
                    regroup(n + 1, 1)
                if n >= 1:
                    quant(n - 1, 2)
                    h_quant(n - 1, (0, 1))
                    second_mm(n - 1, (0, 1))
                if c == 3 and g + 1 < G:
                    x_quant(g + 1)
                load_round(n + 1 + RAW_BUFS)
            else:
                quant(n - 1, 2)
                for h in range(H):
                    mult(n - 1, h)
                    h_quant(n - 1, (h,))
                    second_mm(n - 1, (h,))
                finish(G - 1, 0)
                finish_in_halves(G - 1, 1)
